import numpy as np
import ml_dtypes


def mxq(x, axis, fmt="e4m3"):
    dtype, down = {"e4m3": (ml_dtypes.float8_e4m3fn, 7), "e5m2": (ml_dtypes.float8_e5m2, 14)}[fmt]
    v = np.moveaxis(np.asarray(x, np.float32).astype(ml_dtypes.bfloat16).astype(np.float64), axis, -1)
    blocks = v.reshape(v.shape[:-1] + (-1, 32))
    amax = np.abs(blocks).max(-1, keepdims=True)
    byte = np.maximum(np.where(amax > 0, np.frexp(amax)[1] - 1 + 127, 0) - down, 1)
    scale = np.exp2(byte - 127.0)
    codes = (blocks / scale).astype(np.float32).astype(dtype).astype(np.float64)
    return np.moveaxis((codes * scale).reshape(v.shape), -1, axis)


WIDE = False


def mx_kscale(k):
    if not WIDE:
        return np.ones(k)
    levels = np.array([10, -10, 5, -5, 0])
    if k % 512:
        return np.exp2(np.random.permutation(np.resize(levels, k // 32))).repeat(32)
    a = np.empty((k // 512, 16))
    for p in range(k // 512):
        a[p, :8] = np.random.permutation(np.resize(levels, 8))
        for g in range(8):
            far = levels[np.abs(levels - a[p, g]) >= 10]
            a[p, g + 8] = far[np.random.randint(len(far))]
    return np.exp2(a.ravel()).repeat(32)


BF16 = ml_dtypes.bfloat16


def bf(x):
    return np.asarray(x, np.float32).astype(BF16)


def f64(x):
    return np.asarray(x).astype(np.float64)


E2M1 = np.array([0.0, 0.5, 1.0, 1.5, 2.0, 3.0, 4.0, 6.0, -0.0, -0.5, -1.0, -1.5, -2.0, -3.0, -4.0, -6.0])


def pack_weight(w, fmt):
    k, n = w.shape
    w = f64(bf(w)).reshape(k // 32, 32, n)
    amax = np.abs(w).max(1)
    if fmt == "e4m3":
        byte = np.frexp(amax)[1] - 1 + 127 - 7
    else:
        mant, ex = np.frexp(amax / 6.0)
        byte = np.where(mant > 0.5, ex, ex - 1) + 127
    byte = np.clip(np.where(amax > 0, byte, 1), 1, 254)
    scaled = (w * np.exp2(127.0 - byte)[:, None, :]).reshape(k, n).astype(np.float32)
    by_word = np.ascontiguousarray(scaled.reshape(k // 512, 128, 4, n).transpose(0, 1, 3, 2))
    if fmt == "e4m3":
        words = by_word.astype(ml_dtypes.float8_e4m3fn).view(np.uint8)
    else:
        c = by_word.astype(ml_dtypes.float4_e2m1fn).view(np.uint8) & 0xF
        words = c[..., 0::2] | (c[..., 1::2] << 4)
    return np.ascontiguousarray(words), np.ascontiguousarray(byte.astype(np.uint8).reshape(k // 512, 16, n))


def unpack_weight(words, scales, fmt):
    g, p, n, _ = words.shape
    if fmt == "e4m3":
        vals = np.ascontiguousarray(words).view(ml_dtypes.float8_e4m3fn).astype(np.float64)
    else:
        nib = np.empty((g, p, n, 4), np.uint8)
        nib[..., 0::2] = words & 0xF
        nib[..., 1::2] = words >> 4
        vals = E2M1[nib]
    vals = vals * np.repeat(np.exp2(scales.astype(np.float64) - 127.0), 8, axis=1)[..., None]
    return vals.transpose(0, 1, 3, 2).reshape(g * 512, n)


B, N, NF, ND, NH = 1, 128, 128, 512, 512


def draw0():
    s = mx_kscale(ND)
    t = mx_kscale(NH)
    atom_features = bf(np.random.standard_normal((B, N, NF)))
    distance_matrix = bf(np.random.random((B, N, N, ND)) * s)
    distance_matrix_mask = bf(0.25 + 0.75 * np.random.random((B, N, N)))
    W_cf = bf(np.random.standard_normal((NF, NH)) / np.sqrt(NF) * t)
    W_df_words, W_df_scales = pack_weight(np.random.standard_normal((ND, NH)) * 1.5 / np.sqrt(ND) / s[:, None], "e4m3")
    W_fc_words, W_fc_scales = pack_weight(np.random.standard_normal((NH, NF)) / np.sqrt(NH) / t[:, None], "e4m3")
    return {
        "atom_features": atom_features,
        "distance_matrix": distance_matrix,
        "distance_matrix_mask": distance_matrix_mask,
        "W_cf": W_cf,
        "W_df_words": W_df_words,
        "W_df_scales": W_df_scales,
        "W_fc_words": W_fc_words,
        "W_fc_scales": W_fc_scales,
        "b_cf": bf(np.random.standard_normal(NH) * 0.3 * t),
        "b_df": bf(np.random.standard_normal(NH) * 0.3),
    }


def core(atom_features, distance_matrix, distance_matrix_mask, W_cf, W_df_words, W_df_scales, W_fc_words, W_fc_scales, b_cf, b_df):
    a = f64(atom_features)
    dist_h = (mxq(f64(distance_matrix), 3, "e4m3") @ unpack_weight(W_df_words, W_df_scales, "e4m3")) + f64(b_df)
    atom_h = a @ f64(W_cf) + f64(b_cf)
    gated = dist_h * atom_h[:, None, :, :]
    out = mxq(gated, 3, "e4m3") @ unpack_weight(W_fc_words, W_fc_scales, "e4m3")
    out = out * f64(distance_matrix_mask)[..., None]
    return np.tanh(out).sum(axis=2) + a


def e4m3fn_bytes(y):
    return np.clip(np.asarray(y, np.float64), -448.0, 448.0).astype(np.float32).astype(ml_dtypes.float8_e4m3fn).view(np.uint8)


def e4m3fn_values(b):
    return np.asarray(b, np.uint8).view(ml_dtypes.float8_e4m3fn).astype(np.float64)


def setup_inputs():
    d = draw0()
    x0 = np.asarray(d['distance_matrix']).astype(np.float64)
    s = (np.max(np.abs(x0), axis=(0, 1, 2), keepdims=True) / 448.0).astype(np.float32)
    out = {}
    for k, v in d.items():
        if k == 'distance_matrix':
            out['distance_matrix_bytes'] = e4m3fn_bytes(x0 / s.astype(np.float64))
            out['distance_matrix_scale'] = s
        else:
            out[k] = v
    return out


def reference(atom_features, distance_matrix_bytes, distance_matrix_scale, distance_matrix_mask, W_cf, W_df_words, W_df_scales, W_fc_words, W_fc_scales, b_cf, b_df):
    return core(atom_features, e4m3fn_values(distance_matrix_bytes) * distance_matrix_scale.astype(np.float64), distance_matrix_mask, W_cf, W_df_words, W_df_scales, W_fc_words, W_fc_scales, b_cf, b_df)

@@ -1,0 +1,271 @@
+from contextlib import ExitStack
+
+import concourse.mybir as mybir
+from concourse.masks import make_identity
+
+P = 128
+K = 512
+H = 512
+NF = 128
+PAIRS = 128 * 128
+J_STEP = 4
+STEPS = 128 // J_STEP
+COLS = J_STEP * 128
+J_LOAD = 8
+
+FLOPS = 2 * PAIRS * K * H + 2 * PAIRS * H * NF + 2 * 128 * NF * H
+
+F32 = mybir.dt.float32
+BF16 = mybir.dt.bfloat16
+I32 = mybir.dt.int32
+U32 = mybir.dt.uint32
+U8 = mybir.dt.uint8
+FP8 = mybir.dt.float8_e4m3fn
+FP8X4 = mybir.dt.float8_e4m3fn_x4
+ALU = mybir.AluOpType
+ACT = mybir.ActivationFunctionType
+
+
+def tile_dtnnstep_pa_t_w8_kernel(
+    tc, atom_features, dm_bytes, dm_scale, dm_mask, W_cf, W_df_words, W_df_scales, W_fc_words, W_fc_scales, b_cf, b_df, out
+):
+    nc = tc.nc
+    with ExitStack() as ctx:
+        keep = ctx.enter_context(tc.tile_pool(name="keep", bufs=1))
+        work = ctx.enter_context(tc.tile_pool(name="work", bufs=3))
+        psum = ctx.enter_context(tc.psum_pool(name="psum", bufs=1))
+        ctx.enter_context(tc.manual_schedule())
+
+        scale_rep = keep.tile([P, J_STEP, K], F32, name="scale_rep")
+        raw = [keep.tile([P, J_LOAD * K], U8, name="raw%d" % b, align_bytes=64) for b in range(128 // J_LOAD)]
+        planes = keep.tile([P, H + NF], U8, name="planes", align_bytes=64)
+        wdf_w = keep.tile([P, H * 4], U8, name="wdf_w", align_bytes=64)
+        wdf_c = keep.tile([P, H], I32, name="wdf_c", align_bytes=64)
+        wdf_s = keep.tile([P, H], U8, name="wdf_s", align_bytes=64)
+        wfc_c = keep.tile([P, NF * 4], U8, name="wfc_c", align_bytes=64)
+        wfc_s = keep.tile([P, NF], U8, name="wfc_s", align_bytes=64)
+        atom = keep.tile([P, NF], BF16, name="atom")
+        atom_t = keep.tile([P, 128], BF16, name="atom_t")
+        wcf = keep.tile([P, H], BF16, name="wcf")
+        wcf_p = keep.tile([P, 4, 128], BF16, name="wcf_p")
+        mask = keep.tile([P, 128], BF16, name="mask")
+        mask_f = keep.tile([P, 128], F32, name="mask_f")
+        bc = keep.tile([P, 4], BF16, name="bc")
+        bd = keep.tile([P, 4], BF16, name="bd")
+        bc_f = keep.tile([P, 4], F32, name="bc_f")
+        bd_f = keep.tile([P, 4], F32, name="bd_f")
+        gate = keep.tile([P, 4, 128], F32, name="gate")
+        gate_b = keep.tile([P, 4, 128], F32, name="gate_b")
+        ident = keep.tile([P, 128], F32, name="ident")
+        ident_b = keep.tile([P, 128], BF16, name="ident_b")
+        warm = keep.tile([P, 1], F32, name="warm")
+
+        nc.gpsimd.memset(warm[:], 0.0)
+        nc.vector.memset(planes[:].bitcast(I32), 0)
+        make_identity(nc, ident[:])
+
+        def load(b):
+            src = dm_bytes[0, :, b * J_LOAD : (b + 1) * J_LOAD, :].rearrange("i j k -> i (j k)")
+            nc.sync.dma_start(out=raw[b][:], in_=src)
+
+        half = J_STEP * K
+        src0 = dm_bytes[0, :, 0:J_LOAD, :].rearrange("i j k -> i (j k)")
+        nc.sync.dma_start(out=raw[0][:, 0:half], in_=src0[:, 0:half])
+        nc.scalar.dma_start(out=scale_rep[:, 0, :], in_=dm_scale.rearrange("a b c k -> (a b c k)").partition_broadcast(P))
+        nc.scalar.dma_start(out=atom[:], in_=atom_features[0])
+        nc.scalar.dma_start(out=wcf[:], in_=W_cf)
+        nc.scalar.dma_start(out=bc[:], in_=b_cf.rearrange("(p t) -> p t", t=4))
+        nc.scalar.dma_start(out=bd[:], in_=b_df.rearrange("(p t) -> p t", t=4))
+        nc.scalar.dma_start(out=mask[:], in_=dm_mask[0])
+        nc.sync.dma_start(out=raw[0][:, half:], in_=src0[:, half:])
+        nc.sync.dma_start(out=wdf_w[:], in_=W_df_words[0].rearrange("p n t -> p (n t)"))
+        nc.sync.dma_start(out=wfc_c[:], in_=W_fc_words[0].rearrange("p n t -> p (n t)"))
+        for q in range(4):
+            nc.sync.dma_start(out=planes[32 * q : 32 * q + 4, 0:H].bitcast(I32), in_=W_df_scales[0, 4 * q : 4 * q + 4, :].bitcast(I32))
+            nc.sync.dma_start(out=planes[32 * q : 32 * q + 4, H:].bitcast(I32), in_=W_fc_scales[0, 4 * q : 4 * q + 4, :].bitcast(I32))
+        for b in range(1, 128 // J_LOAD):
+            load(b)
+
+        nc.scalar.activation(out=warm[:], in_=warm[:], func=ACT.Tanh)
+
+        xs, grp, xc, xsc, gp, gg, gc, gs, tn, hid, ox = ({} for n in range(11))
+
+        def widen(s):
+            xs[s] = work.tile([P, J_STEP * K], BF16, name="xs", align_bytes=64)
+            lo = (s % 2) * half
+            src = raw[s // 2]
+            if s == 0:
+                for j in range(J_STEP):
+                    nc.vector.tensor_tensor(
+                        out=xs[s][:, j * K : (j + 1) * K],
+                        in0=src[:, j * K : (j + 1) * K].bitcast(FP8),
+                        in1=scale_rep[:, 0, :],
+                        op=ALU.mult,
+                    )
+                for j in range(1, J_STEP):
+                    nc.vector.tensor_copy(out=scale_rep[:, j, :], in_=scale_rep[:, 0, :])
+            else:
+                nc.vector.tensor_tensor(
+                    out=xs[s][:],
+                    in0=src[:, lo : lo + half].bitcast(FP8),
+                    in1=scale_rep[:].rearrange("p j k -> p (j k)"),
+                    op=ALU.mult,
+                )
+
+        xt = {}
+
+        def turn(s):
+            words = xs[s][:].bitcast(F32)
+            for h in range(2):
+                xt[s, h] = psum.tile([P, 2, 2, 128], F32, name="xt%d" % h)
+                for jj in range(2):
+                    base = (2 * h + jj) * 256
+                    for u in range(2):
+                        nc.tensor.transpose(xt[s, h][:, jj, u, :], words[:, base + u : base + 256 : 2], ident[:])
+
+        def untwist(s):
+            grp[s] = work.tile([P, COLS * 4], BF16, name="grp", align_bytes=64)
+            for h in range(2):
+                nc.scalar.copy(
+                    out=grp[s][:].bitcast(F32)[:, h * 512 : (h + 1) * 512].rearrange("p (j r u) -> p j r u", j=2, u=2),
+                    in_=xt[s, h][:].rearrange("p j u r -> p j r u"),
+                )
+
+        def quant_x(s):
+            xc[s] = work.tile([P, COLS], U32, name="xc", align_bytes=64)
+            xsc[s] = work.tile([P, COLS], U8, name="xsc", align_bytes=64)
+            nc.vector.quantize_mx(out=xc[s][:].bitcast(FP8X4), scales=xsc[s][:], in_=grp[s][:])
+
+        def hidden(s):
+            for t in range(4):
+                hid[s, t] = psum.tile([P, COLS], F32, name="hid%d" % t)
+                nc.tensor.matmul_mx(
+                    out=hid[s, t][:],
+                    lhsT=wdf_c[:, t * 128 : (t + 1) * 128].bitcast(FP8X4),
+                    lhsT_scale=wdf_s[:, t * 128 : (t + 1) * 128],
+                    rhs=xc[s][:].bitcast(FP8X4),
+                    rhs_scale=xsc[s][:],
+                    start=True,
+                    stop=True,
+                )
+
+        def gating(s):
+            gp[s] = work.tile([P, 4, COLS], BF16, name="gp", align_bytes=64)
+            for t in range(4):
+                for jj in range(J_STEP):
+                    j = s * J_STEP + jj
+                    nc.scalar.activation(
+                        out=gp[s][:, t, jj * 128 : (jj + 1) * 128],
+                        in_=hid[s, t][:, jj * 128 : (jj + 1) * 128],
+                        func=ACT.Identity,
+                        scale=gate[:, t, j : j + 1],
+                        bias=gate_b[:, t, j : j + 1],
+                    )
+
+        def weave(s):
+            gg[s] = work.tile([P, COLS * 4], BF16, name="gg", align_bytes=64)
+            nc.vector.tensor_copy(
+                out=gg[s][:].rearrange("p (c i t) -> p c t i", i=4, t=4),
+                in_=gp[s][:].rearrange("p t (c i) -> p c t i", i=4),
+            )
+
+        def quant_g(s):
+            gc[s] = work.tile([P, COLS], U32, name="gc", align_bytes=64)
+            gs[s] = work.tile([P, COLS], U8, name="gs", align_bytes=64)
+            nc.vector.quantize_mx(out=gc[s][:].bitcast(FP8X4), scales=gs[s][:], in_=gg[s][:])
+
+        def project(s):
+            ox[s] = psum.tile([P, J_STEP, NF], F32, name="ox")
+            for jj in range(J_STEP):
+                nc.tensor.matmul_mx(
+                    out=ox[s][:, jj, :],
+                    lhsT=gc[s][:, jj * 128 : (jj + 1) * 128].bitcast(FP8X4),
+                    lhsT_scale=gs[s][:, jj * 128 : (jj + 1) * 128],
+                    rhs=wfc_c[:].bitcast(FP8X4),
+                    rhs_scale=wfc_s[:],
+                    start=True,
+                    stop=True,
+                )
+
+        def squash(s):
+            tn[s] = work.tile([P, J_STEP, NF], F32, name="tn")
+            for jj in range(J_STEP):
+                j = s * J_STEP + jj
+                nc.scalar.activation(out=tn[s][:, jj, :], in_=ox[s][:, jj, :], func=ACT.Tanh, scale=mask_f[:, j : j + 1])
+
+        acc = psum.tile([P, 128], F32, name="acc")
+
+        def add_up(s):
+            for jj in range(J_STEP):
+                nc.tensor.matmul(
+                    acc[:],
+                    lhsT=tn[s][:, jj, :],
+                    rhs=ident[:],
+                    is_transpose=True,
+                    start=(s == 0 and jj == 0),
+                    stop=(s == STEPS - 1 and jj == J_STEP - 1),
+                )
+
+        def prepare():
+            nc.vector.tensor_copy(out=ident_b[:], in_=ident[:])
+            nc.vector.tensor_copy(out=wcf_p[:], in_=wcf[:].rearrange("p (m t) -> p t m", t=4))
+            pt = psum.tile([P, 128], BF16, name="ox")
+            nc.tensor.transpose(pt[:], atom[:], ident_b[:])
+            nc.scalar.copy(out=atom_t[:], in_=pt[:])
+            nc.vector.tensor_copy(out=bc_f[:], in_=bc[:])
+            nc.vector.tensor_copy(out=bd_f[:], in_=bd[:])
+            ga = psum.tile([P, 4, 128], F32, name="ox")
+            for t in range(4):
+                nc.tensor.matmul(ga[:, t, :], lhsT=wcf_p[:, t, :], rhs=atom_t[:], start=True, stop=True)
+            for t in range(4):
+                nc.scalar.activation(out=gate[:, t, :], in_=ga[:, t, :], func=ACT.Identity, bias=bc_f[:, t : t + 1])
+            for t in range(4):
+                nc.vector.tensor_scalar(out=gate_b[:, t, :], in0=gate[:, t, :], scalar1=bd_f[:, t : t + 1], scalar2=None, op0=ALU.mult)
+            nc.vector.tensor_copy(out=mask_f[:], in_=mask[:])
+
+        def permute():
+            nc.vector.tensor_copy(
+                out=wdf_c[:].rearrange("p (t m) -> p t m", t=4), in_=wdf_w[:].bitcast(I32).rearrange("p (m t) -> p t m", t=4)
+            )
+            nc.vector.tensor_copy(
+                out=wdf_s[:].rearrange("p (t m) -> p t m", t=4), in_=planes[:, 0:H].rearrange("p (m t) -> p t m", t=4)
+            )
+            nc.vector.tensor_copy(out=wfc_s[:], in_=planes[:, H:])
+
+        def on(s):
+            return 0 <= s < STEPS
+
+        for s in range(-3, STEPS + 3):
+            if on(s + 3):
+                widen(s + 3)
+            if on(s - 1):
+                project(s - 1)
+            if on(s - 2):
+                add_up(s - 2)
+            if on(s + 2):
+                untwist(s + 2)
+            if on(s + 3):
+                turn(s + 3)
+            if s == -3:
+                prepare()
+                permute()
+            if on(s + 1):
+                gating(s + 1)
+            if on(s - 1):
+                squash(s - 1)
+            if on(s):
+                weave(s)
+            if on(s + 2):
+                quant_x(s + 2)
+            if on(s):
+                quant_g(s)
+            if on(s + 2):
+                hidden(s + 2)
+
+        acc_s = keep.tile([P, 128], F32, name="acc_s")
+        res = keep.tile([P, NF], F32, name="res")
+        nc.vector.tensor_copy(out=acc_s[:], in_=acc[:])
+        fin = psum.tile([P, 128], F32, name="ox")
+        nc.tensor.transpose(fin[:], acc_s[:], ident[:])
+        nc.vector.tensor_tensor(out=res[:], in0=fin[:], in1=atom[:], op=ALU.add)
+        nc.sync.dma_start(out=out[0], in_=res[:])

@@ -36,7 +36,7 @@ def tile_dtnnstep_pa_t_w8_kernel(
         psum = ctx.enter_context(tc.psum_pool(name="psum", bufs=1))
         ctx.enter_context(tc.manual_schedule())
 
-        scale_rep = keep.tile([P, J_STEP, K], F32, name="scale_rep")
+        scale4 = keep.tile([P, 4], F32, name="scale4")
         raw = [keep.tile([P, J_LOAD * K], U8, name="raw%d" % b, align_bytes=64) for b in range(128 // J_LOAD)]
         planes = keep.tile([P, H + NF], U8, name="planes", align_bytes=64)
         wdf_w = keep.tile([P, H * 4], U8, name="wdf_w", align_bytes=64)
@@ -71,7 +71,7 @@ def tile_dtnnstep_pa_t_w8_kernel(
         half = J_STEP * K
         src0 = dm_bytes[0, :, 0:J_LOAD, :].rearrange("i j k -> i (j k)")
         nc.sync.dma_start(out=raw[0][:, 0:half], in_=src0[:, 0:half])
-        nc.scalar.dma_start(out=scale_rep[:, 0, :], in_=dm_scale.rearrange("a b c k -> (a b c k)").partition_broadcast(P))
+        nc.scalar.dma_start(out=scale4[:], in_=dm_scale.rearrange("a b c (p t) -> p (a b c t)", t=4))
         nc.scalar.dma_start(out=atom[:], in_=atom_features[0])
         nc.scalar.dma_start(out=wcf[:], in_=W_cf)
         nc.scalar.dma_start(out=bc[:], in_=b_cf.rearrange("(p t) -> p t", t=4))
@@ -93,42 +93,27 @@ def tile_dtnnstep_pa_t_w8_kernel(
         def widen(s):
             xs[s] = work.tile([P, J_STEP * K], BF16, name="xs", align_bytes=64)
             lo = (s % 2) * half
-            src = raw[s // 2]
-            if s == 0:
-                for j in range(J_STEP):
-                    nc.vector.tensor_tensor(
-                        out=xs[s][:, j * K : (j + 1) * K],
-                        in0=src[:, j * K : (j + 1) * K].bitcast(FP8),
-                        in1=scale_rep[:, 0, :],
-                        op=ALU.mult,
-                    )
-                for j in range(1, J_STEP):
-                    nc.vector.tensor_copy(out=scale_rep[:, j, :], in_=scale_rep[:, 0, :])
-            else:
-                nc.vector.tensor_tensor(
-                    out=xs[s][:],
-                    in0=src[:, lo : lo + half].bitcast(FP8),
-                    in1=scale_rep[:].rearrange("p j k -> p (j k)"),
-                    op=ALU.mult,
-                )
+            nc.scalar.copy(out=xs[s][:], in_=raw[s // 2][:, lo : lo + half].bitcast(FP8))
 
         xt = {}
 
         def turn(s):
             words = xs[s][:].bitcast(F32)
             for h in range(2):
-                xt[s, h] = psum.tile([P, 2, 2, 128], F32, name="xt%d" % h)
+                xt[s, h] = psum.tile([P, 2, 256], F32, name="xt%d" % h)
                 for jj in range(2):
                     base = (2 * h + jj) * 256
                     for u in range(2):
-                        nc.tensor.transpose(xt[s, h][:, jj, u, :], words[:, base + u : base + 256 : 2], ident[:])
+                        nc.tensor.transpose(xt[s, h][:, u, jj * 128 : (jj + 1) * 128], words[:, base + u : base + 256 : 2], ident[:])
 
-        def untwist(s):
+        def scale_out(s):
             grp[s] = work.tile([P, COLS * 4], BF16, name="grp", align_bytes=64)
             for h in range(2):
-                nc.scalar.copy(
-                    out=grp[s][:].bitcast(F32)[:, h * 512 : (h + 1) * 512].rearrange("p (j r u) -> p j r u", j=2, u=2),
-                    in_=xt[s, h][:].rearrange("p j u r -> p j r u"),
+                nc.vector.tensor_tensor(
+                    out=grp[s][:, h * 1024 : (h + 1) * 1024].rearrange("p (c u e) -> p c u e", u=2, e=2),
+                    in0=xt[s, h][:].bitcast(BF16).rearrange("p u (c e) -> p c u e", e=2),
+                    in1=scale4[:].rearrange("p (u e) -> p u e", e=2).unsqueeze(1).to_broadcast([P, 256, 2, 2]),
+                    op=ALU.mult,
                 )
 
         def quant_x(s):
@@ -151,7 +136,16 @@ def tile_dtnnstep_pa_t_w8_kernel(
 
         def gating(s):
             gp[s] = work.tile([P, 4, COLS], BF16, name="gp", align_bytes=64)
-            for t in range(4):
+            for t in range(3, 4):
+                nc.vector.scalar_tensor_tensor(
+                    out=gp[s][:, t, :].rearrange("p (j i) -> p j i", i=128),
+                    in0=hid[s, t][:].rearrange("p (j i) -> p j i", i=128),
+                    scalar=bd_f[:, t : t + 1],
+                    in1=gate[:, t, s * J_STEP : (s + 1) * J_STEP].unsqueeze(2).to_broadcast([P, J_STEP, 128]),
+                    op0=ALU.add,
+                    op1=ALU.mult,
+                )
+            for t in range(3):
                 for jj in range(J_STEP):
                     j = s * J_STEP + jj
                     nc.scalar.activation(
@@ -163,10 +157,14 @@ def tile_dtnnstep_pa_t_w8_kernel(
                     )
 
         def weave(s):
-            gg[s] = work.tile([P, COLS * 4], BF16, name="gg", align_bytes=64)
-            nc.vector.tensor_copy(
-                out=gg[s][:].rearrange("p (c i t) -> p c t i", i=4, t=4),
-                in_=gp[s][:].rearrange("p t (c i) -> p c t i", i=4),
+            gg[s] = work.tile([P, COLS * 4], BF16, name="gg", align_bytes=64, bufs=1)
+            nc.gpsimd.tensor_scalar(
+                out=gg[s][:].rearrange("p (c t) -> p c t", t=4),
+                in0=gp[s][:].rearrange("p t c -> p c t"),
+                scalar1=1.0,
+                scalar2=0.0,
+                op0=ALU.mult,
+                op1=ALU.add,
             )
 
         def quant_g(s):
@@ -243,7 +241,7 @@ def tile_dtnnstep_pa_t_w8_kernel(
             if on(s - 2):
                 add_up(s - 2)
             if on(s + 2):
-                untwist(s + 2)
+                scale_out(s + 2)
             if on(s + 3):
                 turn(s + 3)
             if s == -3:

@@ -25,6 +25,22 @@ FP8X4 = mybir.dt.float8_e4m3fn_x4
 ALU = mybir.AluOpType
 ACT = mybir.ActivationFunctionType
 
+CAST_AHEAD = 5
+TURN_AHEAD = 3
+SCALE_AHEAD = 2
+
+
+def cast_on_scalar(s):
+    return 1 if s == 0 else 4 if s % 4 == 0 or s >= 28 else 3
+
+
+def gate_on_vector(s):
+    return 1
+
+
+def weave_on_gpsimd(s):
+    return 1 if s >= STEPS - 2 else 4
+
 
 def tile_dtnnstep_pa_t_w8_kernel(
     tc, atom_features, dm_bytes, dm_scale, dm_mask, W_cf, W_df_words, W_df_scales, W_fc_words, W_fc_scales, b_cf, b_df, out
@@ -43,7 +59,6 @@ def tile_dtnnstep_pa_t_w8_kernel(
         wdf_c = keep.tile([P, H], I32, name="wdf_c", align_bytes=64)
         wdf_s = keep.tile([P, H], U8, name="wdf_s", align_bytes=64)
         wfc_c = keep.tile([P, NF * 4], U8, name="wfc_c", align_bytes=64)
-        wfc_s = keep.tile([P, NF], U8, name="wfc_s", align_bytes=64)
         atom = keep.tile([P, NF], BF16, name="atom")
         atom_t = keep.tile([P, 128], BF16, name="atom_t")
         wcf = keep.tile([P, H], BF16, name="wcf")
@@ -60,42 +75,51 @@ def tile_dtnnstep_pa_t_w8_kernel(
         ident_b = keep.tile([P, 128], BF16, name="ident_b")
         warm = keep.tile([P, 1], F32, name="warm")
 
-        nc.gpsimd.memset(warm[:], 0.0)
+        nc.vector.memset(warm[:], 0.0)
         nc.vector.memset(planes[:].bitcast(I32), 0)
         make_identity(nc, ident[:])
-
-        def load(b):
-            src = dm_bytes[0, :, b * J_LOAD : (b + 1) * J_LOAD, :].rearrange("i j k -> i (j k)")
-            nc.sync.dma_start(out=raw[b][:], in_=src)
+        make_identity(nc, ident_b[:])
 
         half = J_STEP * K
-        src0 = dm_bytes[0, :, 0:J_LOAD, :].rearrange("i j k -> i (j k)")
-        nc.sync.dma_start(out=raw[0][:, 0:half], in_=src0[:, 0:half])
+
+        def load(b, lo, hi):
+            src = dm_bytes[0, :, b * J_LOAD : (b + 1) * J_LOAD, :].rearrange("i j k -> i (j k)")
+            nc.sync.dma_start(out=raw[b][:, lo:hi], in_=src[:, lo:hi])
+
+        load(0, 0, half)
         nc.scalar.dma_start(out=scale4[:], in_=dm_scale.rearrange("a b c (p t) -> p (a b c t)", t=4))
         nc.scalar.dma_start(out=atom[:], in_=atom_features[0])
         nc.scalar.dma_start(out=wcf[:], in_=W_cf)
         nc.scalar.dma_start(out=bc[:], in_=b_cf.rearrange("(p t) -> p t", t=4))
         nc.scalar.dma_start(out=bd[:], in_=b_df.rearrange("(p t) -> p t", t=4))
         nc.scalar.dma_start(out=mask[:], in_=dm_mask[0])
-        nc.sync.dma_start(out=raw[0][:, half:], in_=src0[:, half:])
+        load(0, half, 2 * half)
         nc.sync.dma_start(out=wdf_w[:], in_=W_df_words[0].rearrange("p n t -> p (n t)"))
-        nc.sync.dma_start(out=wfc_c[:], in_=W_fc_words[0].rearrange("p n t -> p (n t)"))
         for q in range(4):
             nc.sync.dma_start(out=planes[32 * q : 32 * q + 4, 0:H].bitcast(I32), in_=W_df_scales[0, 4 * q : 4 * q + 4, :].bitcast(I32))
             nc.sync.dma_start(out=planes[32 * q : 32 * q + 4, H:].bitcast(I32), in_=W_fc_scales[0, 4 * q : 4 * q + 4, :].bitcast(I32))
+        nc.sync.dma_start(out=wfc_c[:], in_=W_fc_words[0].rearrange("p n t -> p (n t)"))
         for b in range(1, 128 // J_LOAD):
-            load(b)
+            load(b, 0, 2 * half)
 
         nc.scalar.activation(out=warm[:], in_=warm[:], func=ACT.Tanh)
+        nc.gpsimd.tensor_copy(out=bc_f[:], in_=bc[:])
+        nc.gpsimd.tensor_copy(out=bd_f[:], in_=bd[:])
+        nc.gpsimd.tensor_copy(out=wcf_p[:], in_=wcf[:].rearrange("p (m t) -> p t m", t=4))
+        nc.gpsimd.tensor_copy(out=mask_f[:], in_=mask[:])
 
-        xs, grp, xc, xsc, gp, gg, gc, gs, tn, hid, ox = ({} for n in range(11))
+        xs, xt, grp, xc, xsc, gp, gg, gc, gs, tn, hid, ox = ({} for n in range(12))
 
-        def widen(s):
-            xs[s] = work.tile([P, J_STEP * K], BF16, name="xs", align_bytes=64)
-            lo = (s % 2) * half
-            nc.scalar.copy(out=xs[s][:], in_=raw[s // 2][:, lo : lo + half].bitcast(FP8))
-
-        xt = {}
+        def widen(s, on_scalar):
+            if on_scalar:
+                xs[s] = work.tile([P, half], BF16, name="xs", align_bytes=64, bufs=CAST_AHEAD - TURN_AHEAD + 3)
+            cut = cast_on_scalar(s) * K
+            base = (s % 2) * half
+            src = raw[s // 2][:].bitcast(FP8)
+            if on_scalar and cut > 0:
+                nc.scalar.copy(out=xs[s][:, 0:cut], in_=src[:, base : base + cut])
+            if not on_scalar and cut < half:
+                nc.vector.tensor_copy(out=xs[s][:, cut:half], in_=src[:, base + cut : base + half])
 
         def turn(s):
             words = xs[s][:].bitcast(F32)
@@ -136,36 +160,45 @@ def tile_dtnnstep_pa_t_w8_kernel(
 
         def gating(s):
             gp[s] = work.tile([P, 4, COLS], BF16, name="gp", align_bytes=64)
-            for t in range(3, 4):
-                nc.vector.scalar_tensor_tensor(
-                    out=gp[s][:, t, :].rearrange("p (j i) -> p j i", i=128),
-                    in0=hid[s, t][:].rearrange("p (j i) -> p j i", i=128),
-                    scalar=bd_f[:, t : t + 1],
-                    in1=gate[:, t, s * J_STEP : (s + 1) * J_STEP].unsqueeze(2).to_broadcast([P, J_STEP, 128]),
-                    op0=ALU.add,
-                    op1=ALU.mult,
-                )
-            for t in range(3):
-                for jj in range(J_STEP):
-                    j = s * J_STEP + jj
-                    nc.scalar.activation(
-                        out=gp[s][:, t, jj * 128 : (jj + 1) * 128],
-                        in_=hid[s, t][:, jj * 128 : (jj + 1) * 128],
-                        func=ACT.Identity,
-                        scale=gate[:, t, j : j + 1],
-                        bias=gate_b[:, t, j : j + 1],
+            for t in range(4):
+                if t >= 4 - gate_on_vector(s):
+                    nc.vector.scalar_tensor_tensor(
+                        out=gp[s][:, t, :].rearrange("p (j i) -> p j i", i=128),
+                        in0=hid[s, t][:].rearrange("p (j i) -> p j i", i=128),
+                        scalar=bd_f[:, t : t + 1],
+                        in1=gate[:, t, s * J_STEP : (s + 1) * J_STEP].unsqueeze(2).to_broadcast([P, J_STEP, 128]),
+                        op0=ALU.add,
+                        op1=ALU.mult,
                     )
+                else:
+                    for jj in range(J_STEP):
+                        j = s * J_STEP + jj
+                        nc.scalar.activation(
+                            out=gp[s][:, t, jj * 128 : (jj + 1) * 128],
+                            in_=hid[s, t][:, jj * 128 : (jj + 1) * 128],
+                            func=ACT.Identity,
+                            scale=gate[:, t, j : j + 1],
+                            bias=gate_b[:, t, j : j + 1],
+                        )
 
         def weave(s):
-            gg[s] = work.tile([P, COLS * 4], BF16, name="gg", align_bytes=64, bufs=1)
-            nc.gpsimd.tensor_scalar(
-                out=gg[s][:].rearrange("p (c t) -> p c t", t=4),
-                in0=gp[s][:].rearrange("p t c -> p c t"),
-                scalar1=1.0,
-                scalar2=0.0,
-                op0=ALU.mult,
-                op1=ALU.add,
-            )
+            gg[s] = work.tile([P, COLS * 4], BF16, name="gg", align_bytes=64, bufs=2)
+            cut = weave_on_gpsimd(s) * 128
+            part = 256 if cut == COLS else 128
+            for lo in range(0, cut, part):
+                nc.gpsimd.tensor_scalar(
+                    out=gg[s][:, lo * 4 : (lo + part) * 4].rearrange("p (c t) -> p c t", t=4),
+                    in0=gp[s][:, :, lo : lo + part].rearrange("p t c -> p c t"),
+                    scalar1=1.0,
+                    scalar2=0.0,
+                    op0=ALU.mult,
+                    op1=ALU.add,
+                )
+            if cut < COLS:
+                nc.vector.tensor_copy(
+                    out=gg[s][:, cut * 4 :].rearrange("p (c i t) -> p c t i", i=4, t=4),
+                    in_=gp[s][:, :, cut:].rearrange("p t (c i) -> p c t i", i=4),
+                )
 
         def quant_g(s):
             gc[s] = work.tile([P, COLS], U32, name="gc", align_bytes=64)
@@ -180,7 +213,7 @@ def tile_dtnnstep_pa_t_w8_kernel(
                     lhsT=gc[s][:, jj * 128 : (jj + 1) * 128].bitcast(FP8X4),
                     lhsT_scale=gs[s][:, jj * 128 : (jj + 1) * 128],
                     rhs=wfc_c[:].bitcast(FP8X4),
-                    rhs_scale=wfc_s[:],
+                    rhs_scale=planes[:, H:],
                     start=True,
                     stop=True,
                 )
@@ -205,21 +238,16 @@ def tile_dtnnstep_pa_t_w8_kernel(
                 )
 
         def prepare():
-            nc.vector.tensor_copy(out=ident_b[:], in_=ident[:])
-            nc.vector.tensor_copy(out=wcf_p[:], in_=wcf[:].rearrange("p (m t) -> p t m", t=4))
             pt = psum.tile([P, 128], BF16, name="ox")
             nc.tensor.transpose(pt[:], atom[:], ident_b[:])
             nc.scalar.copy(out=atom_t[:], in_=pt[:])
-            nc.vector.tensor_copy(out=bc_f[:], in_=bc[:])
-            nc.vector.tensor_copy(out=bd_f[:], in_=bd[:])
             ga = psum.tile([P, 4, 128], F32, name="ox")
             for t in range(4):
                 nc.tensor.matmul(ga[:, t, :], lhsT=wcf_p[:, t, :], rhs=atom_t[:], start=True, stop=True)
             for t in range(4):
                 nc.scalar.activation(out=gate[:, t, :], in_=ga[:, t, :], func=ACT.Identity, bias=bc_f[:, t : t + 1])
             for t in range(4):
-                nc.vector.tensor_scalar(out=gate_b[:, t, :], in0=gate[:, t, :], scalar1=bd_f[:, t : t + 1], scalar2=None, op0=ALU.mult)
-            nc.vector.tensor_copy(out=mask_f[:], in_=mask[:])
+                nc.scalar.activation(out=gate_b[:, t, :], in_=gate[:, t, :], func=ACT.Copy, scale=bd_f[:, t : t + 1])
 
         def permute():
             nc.vector.tensor_copy(
@@ -228,35 +256,36 @@ def tile_dtnnstep_pa_t_w8_kernel(
             nc.vector.tensor_copy(
                 out=wdf_s[:].rearrange("p (t m) -> p t m", t=4), in_=planes[:, 0:H].rearrange("p (m t) -> p t m", t=4)
             )
-            nc.vector.tensor_copy(out=wfc_s[:], in_=planes[:, H:])
 
         def on(s):
             return 0 <= s < STEPS
 
-        for s in range(-3, STEPS + 3):
-            if on(s + 3):
-                widen(s + 3)
+        for s in range(-CAST_AHEAD, STEPS + 3):
             if on(s - 1):
                 project(s - 1)
             if on(s - 2):
                 add_up(s - 2)
-            if on(s + 2):
-                scale_out(s + 2)
-            if on(s + 3):
-                turn(s + 3)
-            if s == -3:
-                prepare()
+            if on(s + SCALE_AHEAD):
+                scale_out(s + SCALE_AHEAD)
+            if s == -SCALE_AHEAD:
                 permute()
+            if on(s + TURN_AHEAD):
+                turn(s + TURN_AHEAD)
+            if s == -TURN_AHEAD:
+                prepare()
             if on(s + 1):
                 gating(s + 1)
+            if on(s + CAST_AHEAD):
+                widen(s + CAST_AHEAD, True)
             if on(s - 1):
                 squash(s - 1)
+            if on(s + SCALE_AHEAD):
+                quant_x(s + SCALE_AHEAD)
             if on(s):
                 weave(s)
-            if on(s + 2):
-                quant_x(s + 2)
-            if on(s):
                 quant_g(s)
+            if on(s + CAST_AHEAD):
+                widen(s + CAST_AHEAD, False)
             if on(s + 2):
                 hidden(s + 2)
 

@@ -8,10 +8,12 @@ K = 512
 H = 512
 NF = 128
 PAIRS = 128 * 128
-J_STEP = 4
-STEPS = 128 // J_STEP
-COLS = J_STEP * 128
+J_MAX = 4
+COLS = J_MAX * 128
 J_LOAD = 8
+SIZES = [2, 2] + [4] * 31
+STARTS = [sum(SIZES[:s]) for s in range(len(SIZES))]
+STEPS = len(SIZES)
 
 FLOPS = 2 * PAIRS * K * H + 2 * PAIRS * H * NF + 2 * 128 * NF * H
 
@@ -25,21 +27,29 @@ FP8X4 = mybir.dt.float8_e4m3fn_x4
 ALU = mybir.AluOpType
 ACT = mybir.ActivationFunctionType
 
-CAST_AHEAD = 5
-TURN_AHEAD = 3
-SCALE_AHEAD = 2
+CAST_AHEAD = 6
+TURN_AHEAD = 4
+SCALE_AHEAD = 3
+
+
+def share(numerator, denominator, s):
+    return (s + 1) * numerator // denominator - s * numerator // denominator
 
 
 def cast_on_scalar(s):
-    return 1 if s == 0 else 4 if s % 4 == 0 or s >= 28 else 3
+    if SIZES[s] < J_MAX:
+        return 0
+    if s >= STEPS - 8:
+        return 4
+    return share(15, 4, s)
 
 
 def gate_on_vector(s):
-    return 1
+    return 0 if s >= STEPS - 3 else share(5, 4, s)
 
 
 def weave_on_gpsimd(s):
-    return 1 if s >= STEPS - 2 else 4
+    return s < STEPS - 3
 
 
 def tile_dtnnstep_pa_t_w8_kernel(
@@ -80,51 +90,56 @@ def tile_dtnnstep_pa_t_w8_kernel(
         make_identity(nc, ident[:])
         make_identity(nc, ident_b[:])
 
-        half = J_STEP * K
-
         def load(b, lo, hi):
             src = dm_bytes[0, :, b * J_LOAD : (b + 1) * J_LOAD, :].rearrange("i j k -> i (j k)")
             nc.sync.dma_start(out=raw[b][:, lo:hi], in_=src[:, lo:hi])
 
-        load(0, 0, half)
-        nc.scalar.dma_start(out=scale4[:], in_=dm_scale.rearrange("a b c (p t) -> p (a b c t)", t=4))
+        load(0, 0, 2 * K)
+        load(0, 2 * K, 4 * K)
         nc.scalar.dma_start(out=atom[:], in_=atom_features[0])
         nc.scalar.dma_start(out=wcf[:], in_=W_cf)
         nc.scalar.dma_start(out=bc[:], in_=b_cf.rearrange("(p t) -> p t", t=4))
         nc.scalar.dma_start(out=bd[:], in_=b_df.rearrange("(p t) -> p t", t=4))
-        nc.scalar.dma_start(out=mask[:], in_=dm_mask[0])
-        load(0, half, 2 * half)
+        nc.sync.dma_start(out=scale4[:], in_=dm_scale.rearrange("a b c (p t) -> p (a b c t)", t=4))
         nc.sync.dma_start(out=wdf_w[:], in_=W_df_words[0].rearrange("p n t -> p (n t)"))
         for q in range(4):
             nc.sync.dma_start(out=planes[32 * q : 32 * q + 4, 0:H].bitcast(I32), in_=W_df_scales[0, 4 * q : 4 * q + 4, :].bitcast(I32))
+        load(0, 4 * K, 8 * K)
+        load(1, 0, 8 * K)
+        load(2, 0, 8 * K)
+        for q in range(4):
             nc.sync.dma_start(out=planes[32 * q : 32 * q + 4, H:].bitcast(I32), in_=W_fc_scales[0, 4 * q : 4 * q + 4, :].bitcast(I32))
         nc.sync.dma_start(out=wfc_c[:], in_=W_fc_words[0].rearrange("p n t -> p (n t)"))
-        for b in range(1, 128 // J_LOAD):
-            load(b, 0, 2 * half)
+        nc.sync.dma_start(out=mask[:], in_=dm_mask[0])
+        for b in range(3, 128 // J_LOAD):
+            load(b, 0, 8 * K)
 
         nc.scalar.activation(out=warm[:], in_=warm[:], func=ACT.Tanh)
         nc.gpsimd.tensor_copy(out=bc_f[:], in_=bc[:])
         nc.gpsimd.tensor_copy(out=bd_f[:], in_=bd[:])
-        nc.gpsimd.tensor_copy(out=wcf_p[:], in_=wcf[:].rearrange("p (m t) -> p t m", t=4))
         nc.gpsimd.tensor_copy(out=mask_f[:], in_=mask[:])
 
         xs, xt, grp, xc, xsc, gp, gg, gc, gs, tn, hid, ox = ({} for n in range(12))
 
+        def cols(s):
+            return SIZES[s] * 128
+
         def widen(s, on_scalar):
             if on_scalar:
-                xs[s] = work.tile([P, half], BF16, name="xs", align_bytes=64, bufs=CAST_AHEAD - TURN_AHEAD + 3)
-            cut = cast_on_scalar(s) * K
-            base = (s % 2) * half
-            src = raw[s // 2][:].bitcast(FP8)
-            if on_scalar and cut > 0:
-                nc.scalar.copy(out=xs[s][:, 0:cut], in_=src[:, base : base + cut])
-            if not on_scalar and cut < half:
-                nc.vector.tensor_copy(out=xs[s][:, cut:half], in_=src[:, base + cut : base + half])
+                xs[s] = work.tile([P, J_MAX * K], BF16, name="xs", align_bytes=64, bufs=CAST_AHEAD - TURN_AHEAD + 3)
+            cut = (SIZES[s] - cast_on_scalar(s)) * K
+            full = SIZES[s] * K
+            base = (STARTS[s] % J_LOAD) * K
+            src = raw[STARTS[s] // J_LOAD][:].bitcast(FP8)
+            if on_scalar and cut < full:
+                nc.scalar.copy(out=xs[s][:, cut:full], in_=src[:, base + cut : base + full])
+            if not on_scalar and cut > 0:
+                nc.vector.tensor_copy(out=xs[s][:, 0:cut], in_=src[:, base : base + cut])
 
         def turn(s):
             words = xs[s][:].bitcast(F32)
-            for h in range(2):
-                xt[s, h] = psum.tile([P, 2, 256], F32, name="xt%d" % h)
+            for h in range(SIZES[s] // 2):
+                xt[s, h] = psum.tile([P, 2, 256], F32, name="xt%d" % ((STARTS[s] // 2 + h) % 2))
                 for jj in range(2):
                     base = (2 * h + jj) * 256
                     for u in range(2):
@@ -132,7 +147,7 @@ def tile_dtnnstep_pa_t_w8_kernel(
 
         def scale_out(s):
             grp[s] = work.tile([P, COLS * 4], BF16, name="grp", align_bytes=64)
-            for h in range(2):
+            for h in range(SIZES[s] // 2):
                 nc.vector.tensor_tensor(
                     out=grp[s][:, h * 1024 : (h + 1) * 1024].rearrange("p (c u e) -> p c u e", u=2, e=2),
                     in0=xt[s, h][:].bitcast(BF16).rearrange("p u (c e) -> p c u e", e=2),
@@ -141,38 +156,41 @@ def tile_dtnnstep_pa_t_w8_kernel(
                 )
 
         def quant_x(s):
-            xc[s] = work.tile([P, COLS], U32, name="xc", align_bytes=64)
-            xsc[s] = work.tile([P, COLS], U8, name="xsc", align_bytes=64)
-            nc.vector.quantize_mx(out=xc[s][:].bitcast(FP8X4), scales=xsc[s][:], in_=grp[s][:])
+            w = cols(s)
+            xc[s] = work.tile([P, COLS], U32, name="xc", align_bytes=64, bufs=SCALE_AHEAD + 1)
+            xsc[s] = work.tile([P, COLS], U8, name="xsc", align_bytes=64, bufs=SCALE_AHEAD + 1)
+            nc.vector.quantize_mx(out=xc[s][:, 0:w].bitcast(FP8X4), scales=xsc[s][:, 0:w], in_=grp[s][:, 0 : 4 * w])
 
         def hidden(s):
+            w = cols(s)
             for t in range(4):
                 hid[s, t] = psum.tile([P, COLS], F32, name="hid%d" % t)
                 nc.tensor.matmul_mx(
-                    out=hid[s, t][:],
+                    out=hid[s, t][:, 0:w],
                     lhsT=wdf_c[:, t * 128 : (t + 1) * 128].bitcast(FP8X4),
                     lhsT_scale=wdf_s[:, t * 128 : (t + 1) * 128],
-                    rhs=xc[s][:].bitcast(FP8X4),
-                    rhs_scale=xsc[s][:],
+                    rhs=xc[s][:, 0:w].bitcast(FP8X4),
+                    rhs_scale=xsc[s][:, 0:w],
                     start=True,
                     stop=True,
                 )
 
         def gating(s):
+            w = cols(s)
             gp[s] = work.tile([P, 4, COLS], BF16, name="gp", align_bytes=64)
             for t in range(4):
                 if t >= 4 - gate_on_vector(s):
                     nc.vector.scalar_tensor_tensor(
-                        out=gp[s][:, t, :].rearrange("p (j i) -> p j i", i=128),
-                        in0=hid[s, t][:].rearrange("p (j i) -> p j i", i=128),
+                        out=gp[s][:, t, 0:w].rearrange("p (j i) -> p j i", i=128),
+                        in0=hid[s, t][:, 0:w].rearrange("p (j i) -> p j i", i=128),
                         scalar=bd_f[:, t : t + 1],
-                        in1=gate[:, t, s * J_STEP : (s + 1) * J_STEP].unsqueeze(2).to_broadcast([P, J_STEP, 128]),
+                        in1=gate[:, t, STARTS[s] : STARTS[s] + SIZES[s]].unsqueeze(2).to_broadcast([P, SIZES[s], 128]),
                         op0=ALU.add,
                         op1=ALU.mult,
                     )
                 else:
-                    for jj in range(J_STEP):
-                        j = s * J_STEP + jj
+                    for jj in range(SIZES[s]):
+                        j = STARTS[s] + jj
                         nc.scalar.activation(
                             out=gp[s][:, t, jj * 128 : (jj + 1) * 128],
                             in_=hid[s, t][:, jj * 128 : (jj + 1) * 128],
@@ -182,32 +200,32 @@ def tile_dtnnstep_pa_t_w8_kernel(
                         )
 
         def weave(s):
+            w = cols(s)
             gg[s] = work.tile([P, COLS * 4], BF16, name="gg", align_bytes=64, bufs=2)
-            cut = weave_on_gpsimd(s) * 128
-            part = 256 if cut == COLS else 128
-            for lo in range(0, cut, part):
+            if weave_on_gpsimd(s):
                 nc.gpsimd.tensor_scalar(
-                    out=gg[s][:, lo * 4 : (lo + part) * 4].rearrange("p (c t) -> p c t", t=4),
-                    in0=gp[s][:, :, lo : lo + part].rearrange("p t c -> p c t"),
+                    out=gg[s][:, 0 : 4 * w].rearrange("p (c t) -> p c t", t=4),
+                    in0=gp[s][:, :, 0:w].rearrange("p t c -> p c t"),
                     scalar1=1.0,
                     scalar2=0.0,
                     op0=ALU.mult,
                     op1=ALU.add,
                 )
-            if cut < COLS:
+            else:
                 nc.vector.tensor_copy(
-                    out=gg[s][:, cut * 4 :].rearrange("p (c i t) -> p c t i", i=4, t=4),
-                    in_=gp[s][:, :, cut:].rearrange("p t (c i) -> p c t i", i=4),
+                    out=gg[s][:, 0 : 4 * w].rearrange("p (c i t) -> p c t i", i=4, t=4),
+                    in_=gp[s][:, :, 0:w].rearrange("p t (c i) -> p c t i", i=4),
                 )
 
         def quant_g(s):
+            w = cols(s)
             gc[s] = work.tile([P, COLS], U32, name="gc", align_bytes=64)
             gs[s] = work.tile([P, COLS], U8, name="gs", align_bytes=64)
-            nc.vector.quantize_mx(out=gc[s][:].bitcast(FP8X4), scales=gs[s][:], in_=gg[s][:])
+            nc.vector.quantize_mx(out=gc[s][:, 0:w].bitcast(FP8X4), scales=gs[s][:, 0:w], in_=gg[s][:, 0 : 4 * w])
 
         def project(s):
-            ox[s] = psum.tile([P, J_STEP, NF], F32, name="ox")
-            for jj in range(J_STEP):
+            ox[s] = psum.tile([P, J_MAX, NF], F32, name="ox")
+            for jj in range(SIZES[s]):
                 nc.tensor.matmul_mx(
                     out=ox[s][:, jj, :],
                     lhsT=gc[s][:, jj * 128 : (jj + 1) * 128].bitcast(FP8X4),
@@ -219,25 +237,26 @@ def tile_dtnnstep_pa_t_w8_kernel(
                 )
 
         def squash(s):
-            tn[s] = work.tile([P, J_STEP, NF], F32, name="tn")
-            for jj in range(J_STEP):
-                j = s * J_STEP + jj
+            tn[s] = work.tile([P, J_MAX, NF], F32, name="tn")
+            for jj in range(SIZES[s]):
+                j = STARTS[s] + jj
                 nc.scalar.activation(out=tn[s][:, jj, :], in_=ox[s][:, jj, :], func=ACT.Tanh, scale=mask_f[:, j : j + 1])
 
         acc = psum.tile([P, 128], F32, name="acc")
 
         def add_up(s):
-            for jj in range(J_STEP):
+            for jj in range(SIZES[s]):
                 nc.tensor.matmul(
                     acc[:],
                     lhsT=tn[s][:, jj, :],
                     rhs=ident[:],
                     is_transpose=True,
                     start=(s == 0 and jj == 0),
-                    stop=(s == STEPS - 1 and jj == J_STEP - 1),
+                    stop=(s == STEPS - 1 and jj == SIZES[s] - 1),
                 )
 
         def prepare():
+            nc.vector.tensor_copy(out=wcf_p[:], in_=wcf[:].rearrange("p (m t) -> p t m", t=4))
             pt = psum.tile([P, 128], BF16, name="ox")
             nc.tensor.transpose(pt[:], atom[:], ident_b[:])
             nc.scalar.copy(out=atom_t[:], in_=pt[:])
@@ -275,10 +294,10 @@ def tile_dtnnstep_pa_t_w8_kernel(
                 prepare()
             if on(s + 1):
                 gating(s + 1)
-            if on(s + CAST_AHEAD):
-                widen(s + CAST_AHEAD, True)
             if on(s - 1):
                 squash(s - 1)
+            if on(s + CAST_AHEAD):
+                widen(s + CAST_AHEAD, True)
             if on(s + SCALE_AHEAD):
                 quant_x(s + SCALE_AHEAD)
             if on(s):

from contextlib import ExitStack

import concourse.mybir as mybir
from concourse.masks import make_identity

P = 128
K = 512
H = 512
NF = 128
PAIRS = 128 * 128
J_MAX = 4
COLS = J_MAX * 128
J_LOAD = 8
SIZES = [2, 2] + [4] * 31
STARTS = [sum(SIZES[:s]) for s in range(len(SIZES))]
STEPS = len(SIZES)

FLOPS = 2 * PAIRS * K * H + 2 * PAIRS * H * NF + 2 * 128 * NF * H

F32 = mybir.dt.float32
BF16 = mybir.dt.bfloat16
I32 = mybir.dt.int32
U32 = mybir.dt.uint32
U8 = mybir.dt.uint8
FP8 = mybir.dt.float8_e4m3fn
FP8X4 = mybir.dt.float8_e4m3fn_x4
ALU = mybir.AluOpType
ACT = mybir.ActivationFunctionType

CAST_AHEAD = 6
TURN_AHEAD = 4
SCALE_AHEAD = 3


def share(numerator, denominator, s):
    return (s + 1) * numerator // denominator - s * numerator // denominator


def cast_on_scalar(s):
    if SIZES[s] < J_MAX:
        return 0
    if s >= STEPS - 8:
        return 4
    return share(15, 4, s)


def gate_on_vector(s):
    return 0 if s >= STEPS - 3 else share(5, 4, s)


def weave_on_gpsimd(s):
    return s < STEPS - 3


def tile_dtnnstep_pa_t_w8_kernel(
    tc, atom_features, dm_bytes, dm_scale, dm_mask, W_cf, W_df_words, W_df_scales, W_fc_words, W_fc_scales, b_cf, b_df, out
):
    nc = tc.nc
    with ExitStack() as ctx:
        keep = ctx.enter_context(tc.tile_pool(name="keep", bufs=1))
        work = ctx.enter_context(tc.tile_pool(name="work", bufs=3))
        psum = ctx.enter_context(tc.psum_pool(name="psum", bufs=1))
        ctx.enter_context(tc.manual_schedule())

        scale4 = keep.tile([P, 4], F32, name="scale4")
        raw = [keep.tile([P, J_LOAD * K], U8, name="raw%d" % b, align_bytes=64) for b in range(128 // J_LOAD)]
        planes = keep.tile([P, H + NF], U8, name="planes", align_bytes=64)
        wdf_w = keep.tile([P, H * 4], U8, name="wdf_w", align_bytes=64)
        wdf_c = keep.tile([P, H], I32, name="wdf_c", align_bytes=64)
        wdf_s = keep.tile([P, H], U8, name="wdf_s", align_bytes=64)
        wfc_c = keep.tile([P, NF * 4], U8, name="wfc_c", align_bytes=64)
        atom = keep.tile([P, NF], BF16, name="atom")
        atom_t = keep.tile([P, 128], BF16, name="atom_t")
        wcf = keep.tile([P, H], BF16, name="wcf")
        wcf_p = keep.tile([P, 4, 128], BF16, name="wcf_p")
        mask = keep.tile([P, 128], BF16, name="mask")
        mask_f = keep.tile([P, 128], F32, name="mask_f")
        bc = keep.tile([P, 4], BF16, name="bc")
        bd = keep.tile([P, 4], BF16, name="bd")
        bc_f = keep.tile([P, 4], F32, name="bc_f")
        bd_f = keep.tile([P, 4], F32, name="bd_f")
        gate = keep.tile([P, 4, 128], F32, name="gate")
        gate_b = keep.tile([P, 4, 128], F32, name="gate_b")
        ident = keep.tile([P, 128], F32, name="ident")
        ident_b = keep.tile([P, 128], BF16, name="ident_b")
        warm = keep.tile([P, 1], F32, name="warm")

        nc.vector.memset(warm[:], 0.0)
        nc.vector.memset(planes[:].bitcast(I32), 0)
        make_identity(nc, ident[:])
        make_identity(nc, ident_b[:])

        def load(b, lo, hi):
            src = dm_bytes[0, :, b * J_LOAD : (b + 1) * J_LOAD, :].rearrange("i j k -> i (j k)")
            nc.sync.dma_start(out=raw[b][:, lo:hi], in_=src[:, lo:hi])

        load(0, 0, 2 * K)
        load(0, 2 * K, 4 * K)
        nc.scalar.dma_start(out=atom[:], in_=atom_features[0])
        nc.scalar.dma_start(out=wcf[:], in_=W_cf)
        nc.scalar.dma_start(out=bc[:], in_=b_cf.rearrange("(p t) -> p t", t=4))
        nc.scalar.dma_start(out=bd[:], in_=b_df.rearrange("(p t) -> p t", t=4))
        nc.sync.dma_start(out=scale4[:], in_=dm_scale.rearrange("a b c (p t) -> p (a b c t)", t=4))
        nc.sync.dma_start(out=wdf_w[:], in_=W_df_words[0].rearrange("p n t -> p (n t)"))
        for q in range(4):
            nc.sync.dma_start(out=planes[32 * q : 32 * q + 4, 0:H].bitcast(I32), in_=W_df_scales[0, 4 * q : 4 * q + 4, :].bitcast(I32))
        load(0, 4 * K, 8 * K)
        load(1, 0, 8 * K)
        load(2, 0, 8 * K)
        for q in range(4):
            nc.sync.dma_start(out=planes[32 * q : 32 * q + 4, H:].bitcast(I32), in_=W_fc_scales[0, 4 * q : 4 * q + 4, :].bitcast(I32))
        nc.sync.dma_start(out=wfc_c[:], in_=W_fc_words[0].rearrange("p n t -> p (n t)"))
        nc.sync.dma_start(out=mask[:], in_=dm_mask[0])
        for b in range(3, 128 // J_LOAD):
            load(b, 0, 8 * K)

        nc.scalar.activation(out=warm[:], in_=warm[:], func=ACT.Tanh)
        nc.gpsimd.tensor_copy(out=bc_f[:], in_=bc[:])
        nc.gpsimd.tensor_copy(out=bd_f[:], in_=bd[:])
        nc.gpsimd.tensor_copy(out=mask_f[:], in_=mask[:])

        xs, xt, grp, xc, xsc, gp, gg, gc, gs, tn, hid, ox = ({} for n in range(12))

        def cols(s):
            return SIZES[s] * 128

        def widen(s, on_scalar):
            if on_scalar:
                xs[s] = work.tile([P, J_MAX * K], BF16, name="xs", align_bytes=64, bufs=CAST_AHEAD - TURN_AHEAD + 3)
            cut = (SIZES[s] - cast_on_scalar(s)) * K
            full = SIZES[s] * K
            base = (STARTS[s] % J_LOAD) * K
            src = raw[STARTS[s] // J_LOAD][:].bitcast(FP8)
            if on_scalar and cut < full:
                nc.scalar.copy(out=xs[s][:, cut:full], in_=src[:, base + cut : base + full])
            if not on_scalar and cut > 0:
                nc.vector.tensor_copy(out=xs[s][:, 0:cut], in_=src[:, base : base + cut])

        def turn(s):
            words = xs[s][:].bitcast(F32)
            for h in range(SIZES[s] // 2):
                xt[s, h] = psum.tile([P, 2, 256], F32, name="xt%d" % ((STARTS[s] // 2 + h) % 2))
                for jj in range(2):
                    base = (2 * h + jj) * 256
                    for u in range(2):
                        nc.tensor.transpose(xt[s, h][:, u, jj * 128 : (jj + 1) * 128], words[:, base + u : base + 256 : 2], ident[:])

        def scale_out(s):
            grp[s] = work.tile([P, COLS * 4], BF16, name="grp", align_bytes=64)
            for h in range(SIZES[s] // 2):
                nc.vector.tensor_tensor(
                    out=grp[s][:, h * 1024 : (h + 1) * 1024].rearrange("p (c u e) -> p c u e", u=2, e=2),
                    in0=xt[s, h][:].bitcast(BF16).rearrange("p u (c e) -> p c u e", e=2),
                    in1=scale4[:].rearrange("p (u e) -> p u e", e=2).unsqueeze(1).to_broadcast([P, 256, 2, 2]),
                    op=ALU.mult,
                )

        def quant_x(s):
            w = cols(s)
            xc[s] = work.tile([P, COLS], U32, name="xc", align_bytes=64, bufs=SCALE_AHEAD + 1)
            xsc[s] = work.tile([P, COLS], U8, name="xsc", align_bytes=64, bufs=SCALE_AHEAD + 1)
            nc.vector.quantize_mx(out=xc[s][:, 0:w].bitcast(FP8X4), scales=xsc[s][:, 0:w], in_=grp[s][:, 0 : 4 * w])

        def hidden(s):
            w = cols(s)
            for t in range(4):
                hid[s, t] = psum.tile([P, COLS], F32, name="hid%d" % t)
                nc.tensor.matmul_mx(
                    out=hid[s, t][:, 0:w],
                    lhsT=wdf_c[:, t * 128 : (t + 1) * 128].bitcast(FP8X4),
                    lhsT_scale=wdf_s[:, t * 128 : (t + 1) * 128],
                    rhs=xc[s][:, 0:w].bitcast(FP8X4),
                    rhs_scale=xsc[s][:, 0:w],
                    start=True,
                    stop=True,
                )

        def gating(s):
            w = cols(s)
            gp[s] = work.tile([P, 4, COLS], BF16, name="gp", align_bytes=64)
            for t in range(4):
                if t >= 4 - gate_on_vector(s):
                    nc.vector.scalar_tensor_tensor(
                        out=gp[s][:, t, 0:w].rearrange("p (j i) -> p j i", i=128),
                        in0=hid[s, t][:, 0:w].rearrange("p (j i) -> p j i", i=128),
                        scalar=bd_f[:, t : t + 1],
                        in1=gate[:, t, STARTS[s] : STARTS[s] + SIZES[s]].unsqueeze(2).to_broadcast([P, SIZES[s], 128]),
                        op0=ALU.add,
                        op1=ALU.mult,
                    )
                else:
                    for jj in range(SIZES[s]):
                        j = STARTS[s] + jj
                        nc.scalar.activation(
                            out=gp[s][:, t, jj * 128 : (jj + 1) * 128],
                            in_=hid[s, t][:, jj * 128 : (jj + 1) * 128],
                            func=ACT.Identity,
                            scale=gate[:, t, j : j + 1],
                            bias=gate_b[:, t, j : j + 1],
                        )

        def weave(s):
            w = cols(s)
            gg[s] = work.tile([P, COLS * 4], BF16, name="gg", align_bytes=64, bufs=2)
            if weave_on_gpsimd(s):
                nc.gpsimd.tensor_scalar(
                    out=gg[s][:, 0 : 4 * w].rearrange("p (c t) -> p c t", t=4),
                    in0=gp[s][:, :, 0:w].rearrange("p t c -> p c t"),
                    scalar1=1.0,
                    scalar2=0.0,
                    op0=ALU.mult,
                    op1=ALU.add,
                )
            else:
                nc.vector.tensor_copy(
                    out=gg[s][:, 0 : 4 * w].rearrange("p (c i t) -> p c t i", i=4, t=4),
                    in_=gp[s][:, :, 0:w].rearrange("p t (c i) -> p c t i", i=4),
                )

        def quant_g(s):
            w = cols(s)
            gc[s] = work.tile([P, COLS], U32, name="gc", align_bytes=64)
            gs[s] = work.tile([P, COLS], U8, name="gs", align_bytes=64)
            nc.vector.quantize_mx(out=gc[s][:, 0:w].bitcast(FP8X4), scales=gs[s][:, 0:w], in_=gg[s][:, 0 : 4 * w])

        def project(s):
            ox[s] = psum.tile([P, J_MAX, NF], F32, name="ox")
            for jj in range(SIZES[s]):
                nc.tensor.matmul_mx(
                    out=ox[s][:, jj, :],
                    lhsT=gc[s][:, jj * 128 : (jj + 1) * 128].bitcast(FP8X4),
                    lhsT_scale=gs[s][:, jj * 128 : (jj + 1) * 128],
                    rhs=wfc_c[:].bitcast(FP8X4),
                    rhs_scale=planes[:, H:],
                    start=True,
                    stop=True,
                )

        def squash(s):
            tn[s] = work.tile([P, J_MAX, NF], F32, name="tn")
            for jj in range(SIZES[s]):
                j = STARTS[s] + jj
                nc.scalar.activation(out=tn[s][:, jj, :], in_=ox[s][:, jj, :], func=ACT.Tanh, scale=mask_f[:, j : j + 1])

        acc = psum.tile([P, 128], F32, name="acc")

        def add_up(s):
            for jj in range(SIZES[s]):
                nc.tensor.matmul(
                    acc[:],
                    lhsT=tn[s][:, jj, :],
                    rhs=ident[:],
                    is_transpose=True,
                    start=(s == 0 and jj == 0),
                    stop=(s == STEPS - 1 and jj == SIZES[s] - 1),
                )

        def prepare():
            nc.vector.tensor_copy(out=wcf_p[:], in_=wcf[:].rearrange("p (m t) -> p t m", t=4))
            pt = psum.tile([P, 128], BF16, name="ox")
            nc.tensor.transpose(pt[:], atom[:], ident_b[:])
            nc.scalar.copy(out=atom_t[:], in_=pt[:])
            ga = psum.tile([P, 4, 128], F32, name="ox")
            for t in range(4):
                nc.tensor.matmul(ga[:, t, :], lhsT=wcf_p[:, t, :], rhs=atom_t[:], start=True, stop=True)
            for t in range(4):
                nc.scalar.activation(out=gate[:, t, :], in_=ga[:, t, :], func=ACT.Identity, bias=bc_f[:, t : t + 1])
            for t in range(4):
                nc.scalar.activation(out=gate_b[:, t, :], in_=gate[:, t, :], func=ACT.Copy, scale=bd_f[:, t : t + 1])

        def permute():
            nc.vector.tensor_copy(
                out=wdf_c[:].rearrange("p (t m) -> p t m", t=4), in_=wdf_w[:].bitcast(I32).rearrange("p (m t) -> p t m", t=4)
            )
            nc.vector.tensor_copy(
                out=wdf_s[:].rearrange("p (t m) -> p t m", t=4), in_=planes[:, 0:H].rearrange("p (m t) -> p t m", t=4)
            )

        def on(s):
            return 0 <= s < STEPS

        for s in range(-CAST_AHEAD, STEPS + 3):
            if on(s - 1):
                project(s - 1)
            if on(s - 2):
                add_up(s - 2)
            if on(s + SCALE_AHEAD):
                scale_out(s + SCALE_AHEAD)
            if s == -SCALE_AHEAD:
                permute()
            if on(s + TURN_AHEAD):
                turn(s + TURN_AHEAD)
            if s == -TURN_AHEAD:
                prepare()
            if on(s + 1):
                gating(s + 1)
            if on(s - 1):
                squash(s - 1)
            if on(s + CAST_AHEAD):
                widen(s + CAST_AHEAD, True)
            if on(s + SCALE_AHEAD):
                quant_x(s + SCALE_AHEAD)
            if on(s):
                weave(s)
                quant_g(s)
            if on(s + CAST_AHEAD):
                widen(s + CAST_AHEAD, False)
            if on(s + 2):
                hidden(s + 2)

        acc_s = keep.tile([P, 128], F32, name="acc_s")
        res = keep.tile([P, NF], F32, name="res")
        nc.vector.tensor_copy(out=acc_s[:], in_=acc[:])
        fin = psum.tile([P, 128], F32, name="ox")
        nc.tensor.transpose(fin[:], acc_s[:], ident[:])
        nc.vector.tensor_tensor(out=res[:], in0=fin[:], in1=atom[:], op=ALU.add)
        nc.sync.dma_start(out=out[0], in_=res[:])
